import numpy as np
import ml_dtypes


BF16 = ml_dtypes.bfloat16


def bf(x):
    return np.asarray(x, np.float32).astype(BF16)


def f64(x):
    return np.asarray(x).astype(np.float64)


E2M1 = np.array([0.0, 0.5, 1.0, 1.5, 2.0, 3.0, 4.0, 6.0, -0.0, -0.5, -1.0, -1.5, -2.0, -3.0, -4.0, -6.0])


def pack_weight(w, fmt):
    k, n = w.shape
    w = f64(bf(w)).reshape(k // 32, 32, n)
    amax = np.abs(w).max(1)
    if fmt == "e4m3":
        byte = np.frexp(amax)[1] - 1 + 127 - 7
    else:
        mant, ex = np.frexp(amax / 6.0)
        byte = np.where(mant > 0.5, ex, ex - 1) + 127
    byte = np.clip(np.where(amax > 0, byte, 1), 1, 254)
    scaled = (w * np.exp2(127.0 - byte)[:, None, :]).reshape(k, n).astype(np.float32)
    by_word = np.ascontiguousarray(scaled.reshape(k // 512, 128, 4, n).transpose(0, 1, 3, 2))
    if fmt == "e4m3":
        words = by_word.astype(ml_dtypes.float8_e4m3fn).view(np.uint8)
    else:
        c = by_word.astype(ml_dtypes.float4_e2m1fn).view(np.uint8) & 0xF
        words = c[..., 0::2] | (c[..., 1::2] << 4)
    return np.ascontiguousarray(words), np.ascontiguousarray(byte.astype(np.uint8).reshape(k // 512, 16, n))


def unpack_weight(words, scales, fmt):
    g, p, n, _ = words.shape
    if fmt == "e4m3":
        vals = np.ascontiguousarray(words).view(ml_dtypes.float8_e4m3fn).astype(np.float64)
    else:
        nib = np.empty((g, p, n, 4), np.uint8)
        nib[..., 0::2] = words & 0xF
        nib[..., 1::2] = words >> 4
        vals = E2M1[nib]
    vals = vals * np.repeat(np.exp2(scales.astype(np.float64) - 127.0), 8, axis=1)[..., None]
    return vals.transpose(0, 1, 3, 2).reshape(g * 512, n)

def pack4(w):
    words, scales = pack_weight(w, "e2m1")
    return words.reshape(words.shape[0], 128, -1), scales


def unpack4(words, scales):
    return unpack_weight(words.reshape(words.shape[0], 128, -1, 2), scales, "e2m1")


def kspread(k):
    return np.exp2(np.repeat(np.random.randint(-6, 7, k // 32), 32).astype(np.float64))


B, S, E, N_HEAD, MP_NUM, ROTARY_DIM = 2, 128, 2048, 16, 4, 64
HEAD_DIM = E // N_HEAD
LOCAL = E // MP_NUM
ROPE_BASE = 10000.0


def rotate_every_two(x):
    x1 = x[..., 0::2]
    x2 = x[..., 1::2]
    return np.stack((-x2, x1), axis=-1).reshape(x.shape)


def rope(x, sin, cos):
    x_rot = x[..., :ROTARY_DIM]
    x_pass = x[..., ROTARY_DIM:]
    x_rot = x_rot * cos + rotate_every_two(x_rot) * sin
    return np.concatenate([x_rot, x_pass], axis=-1)


def setup_inputs():
    s = kspread(E)
    hidden_states = np.random.standard_normal((B, S, E)) * s
    hidden_states_words, hidden_states_scales = pack4(hidden_states.reshape(B * S, E).T)
    w = np.random.standard_normal((3 * E, E)) / np.sqrt(E) / s[None, :]
    words, scales = pack4(w.T)
    return {"hidden_states_words": hidden_states_words,
            "hidden_states_scales": hidden_states_scales,
            "w_qkv_words": words,
            "w_qkv_scales": scales}


def reference(hidden_states_words, hidden_states_scales, w_qkv_words, w_qkv_scales):
    hs = unpack4(hidden_states_words, hidden_states_scales).T.reshape(B, S, E)
    qkv = hs @ unpack4(w_qkv_words, w_qkv_scales)
    qkv = qkv.reshape(B, S, MP_NUM, 3 * LOCAL)
    q = qkv[..., :LOCAL].reshape(B, S, N_HEAD, HEAD_DIM)
    v = qkv[..., LOCAL:2 * LOCAL].reshape(B, S, N_HEAD, HEAD_DIM)
    k = qkv[..., 2 * LOCAL:].reshape(B, S, N_HEAD, HEAD_DIM)
    inv_freq = 1.0 / (ROPE_BASE ** (np.arange(0, ROTARY_DIM, 2) / ROTARY_DIM))
    freqs = np.arange(S)[:, None] * inv_freq[None, :]
    sin = np.repeat(np.sin(freqs), 2, axis=-1)[None, :, None, :]
    cos = np.repeat(np.cos(freqs), 2, axis=-1)[None, :, None, :]
    q = rope(q, sin, cos)
    k = rope(k, sin, cos)
    return q.transpose(0, 2, 1, 3), k.transpose(0, 2, 1, 3), v.transpose(0, 2, 1, 3)

@@ -1,0 +1,201 @@
+import math
+from contextlib import ExitStack
+
+import concourse.mybir as mybir
+
+FLOPS = 2 * 256 * 2048 * 6144
+
+F32 = mybir.dt.float32
+U8 = mybir.dt.uint8
+I32 = mybir.dt.int32
+FP4X4 = mybir.dt.float4_e2m1fn_x4
+ALU = mybir.AluOpType
+ACT = mybir.ActivationFunctionType
+
+P = 128
+PASSES = 4
+BATCH = 2
+PARITY = 2
+BLOCK = 512
+HEADS = 4
+HEAD_DIM = 128
+ROT = 64
+PAIRS = ROT // 2
+N_BLOCKS = 12
+CHUNKS = ((0, 2), (2, 3), (5, 3), (8, 4))
+RUN_SPLIT = (2, 2, 2, 1)
+BLOCK_ORDER = (0, 1, 2, 3, 4, 5, 6, 7, 8, 9, 11, 10)
+
+
+def load_scale_rows(nc, plane, scales, split):
+    step = PASSES // split
+    for g0 in range(0, PASSES, step):
+        for r in range(4):
+            nc.sync.dma_start(
+                out=plane[r:P:32, g0 : g0 + step, :].bitcast(I32),
+                in_=scales[g0 : g0 + step, r:16:4, :].rearrange("g q n -> q g n").bitcast(I32),
+            )
+
+
+def tile_ttcodegenattention_pa_kernel(
+    tc, x_words, x_scales, w_words, w_scales, out_q, out_k, out_v
+):
+    nc = tc.nc
+    with ExitStack() as ctx:
+        keep = ctx.enter_context(tc.tile_pool(name="keep", bufs=1))
+        outs = ctx.enter_context(tc.tile_pool(name="outs", bufs=N_BLOCKS))
+        work = ctx.enter_context(tc.tile_pool(name="work", bufs=4))
+        psum = ctx.enter_context(tc.psum_pool(name="psum", bufs=8))
+        ctx.enter_context(tc.manual_schedule())
+
+        x_codes_in = keep.tile([P, PASSES, 2 * BATCH * P], U8, name="x_codes_in", align_bytes=64)
+        x_plane_in = keep.tile([P, PASSES, BATCH * P], U8, name="x_plane_in", align_bytes=64)
+        x_codes = keep.tile([P, PARITY, PASSES, 2 * P], U8, name="x_codes", align_bytes=64)
+        x_plane = keep.tile([P, PARITY, PASSES, P], U8, name="x_plane", align_bytes=64)
+        w_codes = []
+        w_plane = []
+        for c, (first, n) in enumerate(CHUNKS):
+            wc = keep.tile([P, PASSES, 2 * BLOCK * n], U8, name="w_codes%d" % c, align_bytes=64)
+            wp = keep.tile([P, PASSES, BLOCK * n], U8, name="w_plane%d" % c, align_bytes=64)
+            w_codes.append(wc)
+            w_plane.append(wp)
+
+        zero = keep.tile([P, 1], F32, name="zero")
+        warm = keep.tile([P, 1], F32, name="warm")
+        part = keep.tile([P, 1], I32, name="part")
+        half = keep.tile([P, 1], I32, name="half")
+        angle = keep.tile([P, PARITY, PAIRS], F32, name="angle")
+        fold = keep.tile([P, 2, PARITY, PAIRS], F32, name="fold")
+        cos_tab = keep.tile([P, PARITY, PAIRS, 2], F32, name="cos_tab")
+        sin_tab = keep.tile([P, 2, PARITY, PAIRS], F32, name="sin_tab")
+
+        nc.gpsimd.iota(part[:], pattern=[[0, 1]], base=0, channel_multiplier=1)
+        nc.gpsimd.memset(zero[:], 0.0)
+
+        nc.vector.memset(x_plane_in[:].bitcast(I32), 0)
+        nc.vector.memset(w_plane[0][:].bitcast(I32), 0)
+        nc.vector.tensor_scalar(out=half[:], in0=part[:], scalar1=1, scalar2=None, op0=ALU.arith_shift_right)
+        for e in range(PARITY):
+            nc.vector.tensor_scalar(
+                out=angle[:, e, 0:1], in0=half[:], scalar1=2.0, scalar2=float(e), op0=ALU.mult, op1=ALU.add
+            )
+        nc.vector.memset(w_plane[1][:].bitcast(I32), 0)
+
+        def load_codes(c):
+            first, n = CHUNKS[c]
+            nc.sync.dma_start(
+                out=w_codes[c][:].bitcast(I32),
+                in_=w_words[:, :, 2 * BLOCK * first : 2 * BLOCK * (first + n)]
+                .rearrange("g p n -> p g n")
+                .bitcast(I32),
+            )
+
+        def load_scales(c):
+            first, n = CHUNKS[c]
+            load_scale_rows(
+                nc, w_plane[c], w_scales[:, :, BLOCK * first : BLOCK * (first + n)], RUN_SPLIT[c]
+            )
+
+        nc.sync.dma_start(
+            out=x_codes_in[:].bitcast(I32), in_=x_words.rearrange("g p n -> p g n").bitcast(I32)
+        )
+        load_scale_rows(nc, x_plane_in, x_scales, 1)
+        load_codes(0)
+        load_scales(0)
+        load_codes(1)
+        load_scales(1)
+        load_codes(2)
+
+        for g in range(PASSES):
+            nc.vector.tensor_copy(
+                out=x_plane[:, :, g, :].rearrange("p e (q b) -> p b q e", b=BATCH),
+                in_=x_plane_in[:, g, :].rearrange("p (b q e) -> p b q e", b=BATCH, e=PARITY),
+            )
+            for b in range(BATCH):
+                nc.vector.tensor_copy(
+                    out=x_codes[:, :, g, :].rearrange("p e (q b y) -> p b q e y", b=BATCH, y=2)[:, b],
+                    in_=x_codes_in[:, g, 2 * P * b : 2 * P * (b + 1)].rearrange(
+                        "p (q e y) -> p q e y", e=PARITY, y=2
+                    ),
+                )
+
+        for c in (2, 3):
+            nc.vector.memset(w_plane[c][:].bitcast(I32), 0)
+        load_scales(2)
+        load_codes(3)
+        load_scales(3)
+
+        nc.scalar.activation(out=warm[:], in_=zero[:], func=ACT.Sin)
+        ratio = 10000.0 ** (-1.0 / PAIRS)
+        width = 1
+        while width < PAIRS:
+            nc.scalar.activation(
+                out=angle[:, :, width : 2 * width], in_=angle[:, :, 0:width], func=ACT.Copy,
+                scale=ratio ** width,
+            )
+            width *= 2
+        nc.scalar.activation(
+            out=fold[:, 0], in_=angle[:], func=ACT.Abs, bias=1.5 * math.pi - 32.0 * math.pi, scale=1.0
+        )
+        nc.scalar.activation(out=fold[:, 1], in_=angle[:], func=ACT.Abs, bias=-32.0 * math.pi, scale=1.0)
+        for half_range in (16.0, 8.0, 4.0, 2.0, 1.0):
+            nc.scalar.activation(
+                out=fold[:], in_=fold[:], func=ACT.Abs, bias=-half_range * math.pi, scale=1.0
+            )
+        nc.scalar.activation(
+            out=cos_tab[:], in_=fold[:, 1].unsqueeze(3).to_broadcast([P, PARITY, PAIRS, 2]),
+            func=ACT.Sin, bias=-0.5 * math.pi, scale=1.0,
+        )
+        nc.scalar.activation(out=sin_tab[:, 0], in_=fold[:, 0], func=ACT.Sin, bias=0.5 * math.pi, scale=-1.0)
+        nc.scalar.activation(out=sin_tab[:, 1], in_=fold[:, 0], func=ACT.Sin, bias=-0.5 * math.pi, scale=1.0)
+
+        chunk_of = {}
+        for c, (first, n) in enumerate(CHUNKS):
+            for k in range(n):
+                chunk_of[first + k] = (c, k)
+
+        for j in BLOCK_ORDER:
+            c, k = chunk_of[j]
+            shard, kind = divmod(j, 3)
+            dest = (out_q, out_v, out_k)[kind]
+            res = outs.tile([P, HEADS, PARITY, HEAD_DIM], F32, name="res")
+            for e in range(PARITY):
+                acc = psum.tile([P, BLOCK], F32, name="acc")
+                for g in range(PASSES):
+                    nc.tensor.matmul_mx(
+                        out=acc[:],
+                        lhsT=x_codes[:, e, g, :].bitcast(FP4X4),
+                        lhsT_scale=x_plane[:, e, g, :],
+                        rhs=w_codes[c][:, g, 2 * BLOCK * k : 2 * BLOCK * (k + 1)].bitcast(FP4X4),
+                        rhs_scale=w_plane[c][:, g, BLOCK * k : BLOCK * (k + 1)],
+                        start=(g == 0),
+                        stop=(g == PASSES - 1),
+                    )
+                x = acc[:].rearrange("p (h c) -> p h c", h=HEADS)
+                if kind == 1:
+                    if j == BLOCK_ORDER[-1] and e == 1:
+                        nc.vector.tensor_copy(out=res[:, :, e, :], in_=x)
+                    else:
+                        nc.scalar.copy(out=res[:, :, e, :], in_=x)
+                else:
+                    cos_b = (
+                        cos_tab[:, e].rearrange("p i x -> p (i x)").unsqueeze(1).to_broadcast([P, HEADS, ROT])
+                    )
+                    nsin_b = sin_tab[:, 0, e, :].unsqueeze(1).to_broadcast([P, HEADS, PAIRS])
+                    psin_b = sin_tab[:, 1, e, :].unsqueeze(1).to_broadcast([P, HEADS, PAIRS])
+                    cross = work.tile([P, HEADS, 2, PAIRS], F32, name="cross")
+                    nc.scalar.copy(out=res[:, :, e, ROT:HEAD_DIM], in_=x[:, :, ROT:HEAD_DIM])
+                    nc.vector.tensor_tensor(out=res[:, :, e, 0:ROT], in0=x[:, :, 0:ROT], in1=cos_b, op=ALU.mult)
+                    nc.vector.tensor_tensor(out=cross[:, :, 0, :], in0=x[:, :, 1:ROT:2], in1=nsin_b, op=ALU.mult)
+                    nc.vector.tensor_tensor(out=cross[:, :, 1, :], in0=x[:, :, 0:ROT:2], in1=psin_b, op=ALU.mult)
+                    rot = res[:, :, e, 0:ROT].rearrange("p h (i x) -> p h i x", x=2)
+                    nc.vector.tensor_tensor(
+                        out=rot, in0=rot, in1=cross[:].rearrange("p h x i -> p h i x"), op=ALU.add
+                    )
+            for b in range(BATCH):
+                nc.sync.dma_start(
+                    out=dest[b, HEADS * shard : HEADS * (shard + 1), :, :].rearrange(
+                        "h (q e) c -> q h (e c)", e=PARITY
+                    ),
+                    in_=res[b:P:BATCH].rearrange("p h e c -> p h (e c)"),
+                )

@@ -23,18 +23,14 @@ ROT = 64
 PAIRS = ROT // 2
 N_BLOCKS = 12
 CHUNKS = ((0, 2), (2, 3), (5, 3), (8, 4))
-RUN_SPLIT = (2, 2, 2, 1)
 BLOCK_ORDER = (0, 1, 2, 3, 4, 5, 6, 7, 8, 9, 11, 10)
 
 
-def load_scale_rows(nc, plane, scales, split):
-    step = PASSES // split
-    for g0 in range(0, PASSES, step):
-        for r in range(4):
-            nc.sync.dma_start(
-                out=plane[r:P:32, g0 : g0 + step, :].bitcast(I32),
-                in_=scales[g0 : g0 + step, r:16:4, :].rearrange("g q n -> q g n").bitcast(I32),
-            )
+def load_scale_rows(nc, plane, scales, r):
+    nc.sync.dma_start(
+        out=plane[r:P:32, :, :].bitcast(I32),
+        in_=scales[:, r:16:4, :].rearrange("g q n -> q g n").bitcast(I32),
+    )
 
 
 def tile_ttcodegenattention_pa_kernel(
@@ -81,30 +77,22 @@ def tile_ttcodegenattention_pa_kernel(
             )
         nc.vector.memset(w_plane[1][:].bitcast(I32), 0)
 
-        def load_codes(c):
+        def load_chunk(c):
             first, n = CHUNKS[c]
-            nc.sync.dma_start(
-                out=w_codes[c][:].bitcast(I32),
-                in_=w_words[:, :, 2 * BLOCK * first : 2 * BLOCK * (first + n)]
-                .rearrange("g p n -> p g n")
-                .bitcast(I32),
-            )
-
-        def load_scales(c):
-            first, n = CHUNKS[c]
-            load_scale_rows(
-                nc, w_plane[c], w_scales[:, :, BLOCK * first : BLOCK * (first + n)], RUN_SPLIT[c]
-            )
+            for g in range(PASSES):
+                nc.sync.dma_start(
+                    out=w_codes[c][:, g, :].bitcast(I32),
+                    in_=w_words[g, :, 2 * BLOCK * first : 2 * BLOCK * (first + n)].bitcast(I32),
+                )
+                load_scale_rows(nc, w_plane[c], w_scales[:, :, BLOCK * first : BLOCK * (first + n)], g)
 
         nc.sync.dma_start(
             out=x_codes_in[:].bitcast(I32), in_=x_words.rearrange("g p n -> p g n").bitcast(I32)
         )
-        load_scale_rows(nc, x_plane_in, x_scales, 1)
-        load_codes(0)
-        load_scales(0)
-        load_codes(1)
-        load_scales(1)
-        load_codes(2)
+        for r in range(4):
+            load_scale_rows(nc, x_plane_in, x_scales, r)
+        load_chunk(0)
+        load_chunk(1)
 
         for g in range(PASSES):
             nc.vector.tensor_copy(
@@ -121,9 +109,8 @@ def tile_ttcodegenattention_pa_kernel(
 
         for c in (2, 3):
             nc.vector.memset(w_plane[c][:].bitcast(I32), 0)
-        load_scales(2)
-        load_codes(3)
-        load_scales(3)
+        load_chunk(2)
+        load_chunk(3)
 
         nc.scalar.activation(out=warm[:], in_=zero[:], func=ACT.Sin)
         ratio = 10000.0 ** (-1.0 / PAIRS)

@@ -77,14 +77,17 @@ def tile_ttcodegenattention_pa_kernel(
             )
         nc.vector.memset(w_plane[1][:].bitcast(I32), 0)
 
-        def load_chunk(c):
+        def load_quarter(c, g):
             first, n = CHUNKS[c]
+            nc.sync.dma_start(
+                out=w_codes[c][:, g, :].bitcast(I32),
+                in_=w_words[g, :, 2 * BLOCK * first : 2 * BLOCK * (first + n)].bitcast(I32),
+            )
+            load_scale_rows(nc, w_plane[c], w_scales[:, :, BLOCK * first : BLOCK * (first + n)], g)
+
+        def load_chunk(c):
             for g in range(PASSES):
-                nc.sync.dma_start(
-                    out=w_codes[c][:, g, :].bitcast(I32),
-                    in_=w_words[g, :, 2 * BLOCK * first : 2 * BLOCK * (first + n)].bitcast(I32),
-                )
-                load_scale_rows(nc, w_plane[c], w_scales[:, :, BLOCK * first : BLOCK * (first + n)], g)
+                load_quarter(c, g)
 
         nc.sync.dma_start(
             out=x_codes_in[:].bitcast(I32), in_=x_words.rearrange("g p n -> p g n").bitcast(I32)
@@ -110,7 +113,6 @@ def tile_ttcodegenattention_pa_kernel(
         for c in (2, 3):
             nc.vector.memset(w_plane[c][:].bitcast(I32), 0)
         load_chunk(2)
-        load_chunk(3)
 
         nc.scalar.activation(out=warm[:], in_=zero[:], func=ACT.Sin)
         ratio = 10000.0 ** (-1.0 / PAIRS)
@@ -141,6 +143,15 @@ def tile_ttcodegenattention_pa_kernel(
             for k in range(n):
                 chunk_of[first + k] = (c, k)
 
+        def store(dest, shard, res, b):
+            nc.sync.dma_start(
+                out=dest[b, HEADS * shard : HEADS * (shard + 1), :, :].rearrange(
+                    "h (q e) c -> q h (e c)", e=PARITY
+                ),
+                in_=res[b:P:BATCH].rearrange("p h e c -> p h (e c)"),
+            )
+
+        held = []
         for j in BLOCK_ORDER:
             c, k = chunk_of[j]
             shard, kind = divmod(j, 3)
@@ -179,10 +190,13 @@ def tile_ttcodegenattention_pa_kernel(
                     nc.vector.tensor_tensor(
                         out=rot, in0=rot, in1=cross[:].rearrange("p h x i -> p h i x"), op=ALU.add
                     )
-            for b in range(BATCH):
-                nc.sync.dma_start(
-                    out=dest[b, HEADS * shard : HEADS * (shard + 1), :, :].rearrange(
-                        "h (q e) c -> q h (e c)", e=PARITY
-                    ),
-                    in_=res[b:P:BATCH].rearrange("p h e c -> p h (e c)"),
-                )
+            if j in BLOCK_ORDER[0:2]:
+                held.append((dest, shard, res))
+                if len(held) == 2:
+                    for g in range(PASSES):
+                        load_quarter(3, g)
+                        held_dest, held_shard, held_res = held[g // BATCH]
+                        store(held_dest, held_shard, held_res, g % BATCH)
+            else:
+                for b in range(BATCH):
+                    store(dest, shard, res, b)

@@ -44,15 +44,15 @@ def tile_ttcodegenattention_pa_kernel(
         psum = ctx.enter_context(tc.psum_pool(name="psum", bufs=8))
         ctx.enter_context(tc.manual_schedule())
 
-        x_codes_in = keep.tile([P, PASSES, 2 * BATCH * P], U8, name="x_codes_in", align_bytes=64)
-        x_plane_in = keep.tile([P, PASSES, BATCH * P], U8, name="x_plane_in", align_bytes=64)
+        x_codes_in = keep.tile([P, PASSES, 2 * BATCH * P], U8, name="x_codes_in", align_bytes=256)
+        x_plane_in = keep.tile([P, PASSES, BATCH * P], U8, name="x_plane_in", align_bytes=256)
         x_codes = keep.tile([P, PARITY, PASSES, 2 * P], U8, name="x_codes", align_bytes=64)
         x_plane = keep.tile([P, PARITY, PASSES, P], U8, name="x_plane", align_bytes=64)
         w_codes = []
         w_plane = []
         for c, (first, n) in enumerate(CHUNKS):
-            wc = keep.tile([P, PASSES, 2 * BLOCK * n], U8, name="w_codes%d" % c, align_bytes=64)
-            wp = keep.tile([P, PASSES, BLOCK * n], U8, name="w_plane%d" % c, align_bytes=64)
+            wc = keep.tile([P, PASSES, 2 * BLOCK * n], U8, name="w_codes%d" % c, align_bytes=256)
+            wp = keep.tile([P, PASSES, BLOCK * n], U8, name="w_plane%d" % c, align_bytes=256)
             w_codes.append(wc)
             w_plane.append(wp)
 
@@ -156,7 +156,7 @@ def tile_ttcodegenattention_pa_kernel(
             c, k = chunk_of[j]
             shard, kind = divmod(j, 3)
             dest = (out_q, out_v, out_k)[kind]
-            res = outs.tile([P, HEADS, PARITY, HEAD_DIM], F32, name="res")
+            res = outs.tile([P, HEADS, PARITY, HEAD_DIM], F32, name="res", align_bytes=256)
             for e in range(PARITY):
                 acc = psum.tile([P, BLOCK], F32, name="acc")
                 for g in range(PASSES):

@@ -187,7 +187,7 @@ def tile_ttcodegenattention_pa_kernel(
                     nc.vector.tensor_tensor(out=cross[:, :, 0, :], in0=x[:, :, 1:ROT:2], in1=nsin_b, op=ALU.mult)
                     nc.vector.tensor_tensor(out=cross[:, :, 1, :], in0=x[:, :, 0:ROT:2], in1=psin_b, op=ALU.mult)
                     rot = res[:, :, e, 0:ROT].rearrange("p h (i x) -> p h i x", x=2)
-                    nc.vector.tensor_tensor(
+                    nc.gpsimd.tensor_tensor(
                         out=rot, in0=rot, in1=cross[:].rearrange("p h x i -> p h i x"), op=ALU.add
                     )
             if j in BLOCK_ORDER[0:2]:

@@ -44,15 +44,15 @@ def tile_ttcodegenattention_pa_kernel(
         psum = ctx.enter_context(tc.psum_pool(name="psum", bufs=8))
         ctx.enter_context(tc.manual_schedule())
 
-        x_codes_in = keep.tile([P, PASSES, 2 * BATCH * P], U8, name="x_codes_in", align_bytes=256)
-        x_plane_in = keep.tile([P, PASSES, BATCH * P], U8, name="x_plane_in", align_bytes=256)
+        x_codes_in = keep.tile([P, PASSES, 2 * BATCH * P], U8, name="x_codes_in", align_bytes=1024)
+        x_plane_in = keep.tile([P, PASSES, BATCH * P], U8, name="x_plane_in", align_bytes=1024)
         x_codes = keep.tile([P, PARITY, PASSES, 2 * P], U8, name="x_codes", align_bytes=64)
         x_plane = keep.tile([P, PARITY, PASSES, P], U8, name="x_plane", align_bytes=64)
         w_codes = []
         w_plane = []
         for c, (first, n) in enumerate(CHUNKS):
-            wc = keep.tile([P, PASSES, 2 * BLOCK * n], U8, name="w_codes%d" % c, align_bytes=256)
-            wp = keep.tile([P, PASSES, BLOCK * n], U8, name="w_plane%d" % c, align_bytes=256)
+            wc = keep.tile([P, PASSES, 2 * BLOCK * n], U8, name="w_codes%d" % c, align_bytes=4096)
+            wp = keep.tile([P, PASSES, BLOCK * n], U8, name="w_plane%d" % c, align_bytes=1024)
             w_codes.append(wc)
             w_plane.append(wp)
 
@@ -156,7 +156,7 @@ def tile_ttcodegenattention_pa_kernel(
             c, k = chunk_of[j]
             shard, kind = divmod(j, 3)
             dest = (out_q, out_v, out_k)[kind]
-            res = outs.tile([P, HEADS, PARITY, HEAD_DIM], F32, name="res", align_bytes=256)
+            res = outs.tile([P, HEADS, PARITY, HEAD_DIM], F32, name="res", align_bytes=4096)
             for e in range(PARITY):
                 acc = psum.tile([P, BLOCK], F32, name="acc")
                 for g in range(PASSES):

import math
from contextlib import ExitStack

import concourse.mybir as mybir

FLOPS = 2 * 256 * 2048 * 6144

F32 = mybir.dt.float32
U8 = mybir.dt.uint8
I32 = mybir.dt.int32
FP4X4 = mybir.dt.float4_e2m1fn_x4
ALU = mybir.AluOpType
ACT = mybir.ActivationFunctionType

P = 128
PASSES = 4
BATCH = 2
PARITY = 2
BLOCK = 512
HEADS = 4
HEAD_DIM = 128
ROT = 64
PAIRS = ROT // 2
N_BLOCKS = 12
CHUNKS = ((0, 2), (2, 3), (5, 3), (8, 4))
BLOCK_ORDER = (0, 1, 2, 3, 4, 5, 6, 7, 8, 9, 11, 10)


def load_scale_rows(nc, plane, scales, r):
    nc.sync.dma_start(
        out=plane[r:P:32, :, :].bitcast(I32),
        in_=scales[:, r:16:4, :].rearrange("g q n -> q g n").bitcast(I32),
    )


def tile_ttcodegenattention_pa_kernel(
    tc, x_words, x_scales, w_words, w_scales, out_q, out_k, out_v
):
    nc = tc.nc
    with ExitStack() as ctx:
        keep = ctx.enter_context(tc.tile_pool(name="keep", bufs=1))
        outs = ctx.enter_context(tc.tile_pool(name="outs", bufs=N_BLOCKS))
        work = ctx.enter_context(tc.tile_pool(name="work", bufs=4))
        psum = ctx.enter_context(tc.psum_pool(name="psum", bufs=8))
        ctx.enter_context(tc.manual_schedule())

        x_codes_in = keep.tile([P, PASSES, 2 * BATCH * P], U8, name="x_codes_in", align_bytes=1024)
        x_plane_in = keep.tile([P, PASSES, BATCH * P], U8, name="x_plane_in", align_bytes=1024)
        x_codes = keep.tile([P, PARITY, PASSES, 2 * P], U8, name="x_codes", align_bytes=64)
        x_plane = keep.tile([P, PARITY, PASSES, P], U8, name="x_plane", align_bytes=64)
        w_codes = []
        w_plane = []
        for c, (first, n) in enumerate(CHUNKS):
            wc = keep.tile([P, PASSES, 2 * BLOCK * n], U8, name="w_codes%d" % c, align_bytes=4096)
            wp = keep.tile([P, PASSES, BLOCK * n], U8, name="w_plane%d" % c, align_bytes=1024)
            w_codes.append(wc)
            w_plane.append(wp)

        zero = keep.tile([P, 1], F32, name="zero")
        warm = keep.tile([P, 1], F32, name="warm")
        part = keep.tile([P, 1], I32, name="part")
        half = keep.tile([P, 1], I32, name="half")
        angle = keep.tile([P, PARITY, PAIRS], F32, name="angle")
        fold = keep.tile([P, 2, PARITY, PAIRS], F32, name="fold")
        cos_tab = keep.tile([P, PARITY, PAIRS, 2], F32, name="cos_tab")
        sin_tab = keep.tile([P, 2, PARITY, PAIRS], F32, name="sin_tab")

        nc.gpsimd.iota(part[:], pattern=[[0, 1]], base=0, channel_multiplier=1)
        nc.gpsimd.memset(zero[:], 0.0)

        nc.vector.memset(x_plane_in[:].bitcast(I32), 0)
        nc.vector.memset(w_plane[0][:].bitcast(I32), 0)
        nc.vector.tensor_scalar(out=half[:], in0=part[:], scalar1=1, scalar2=None, op0=ALU.arith_shift_right)
        for e in range(PARITY):
            nc.vector.tensor_scalar(
                out=angle[:, e, 0:1], in0=half[:], scalar1=2.0, scalar2=float(e), op0=ALU.mult, op1=ALU.add
            )
        nc.vector.memset(w_plane[1][:].bitcast(I32), 0)

        def load_quarter(c, g):
            first, n = CHUNKS[c]
            nc.sync.dma_start(
                out=w_codes[c][:, g, :].bitcast(I32),
                in_=w_words[g, :, 2 * BLOCK * first : 2 * BLOCK * (first + n)].bitcast(I32),
            )
            load_scale_rows(nc, w_plane[c], w_scales[:, :, BLOCK * first : BLOCK * (first + n)], g)

        def load_chunk(c):
            for g in range(PASSES):
                load_quarter(c, g)

        nc.sync.dma_start(
            out=x_codes_in[:].bitcast(I32), in_=x_words.rearrange("g p n -> p g n").bitcast(I32)
        )
        for r in range(4):
            load_scale_rows(nc, x_plane_in, x_scales, r)
        load_chunk(0)
        load_chunk(1)

        for g in range(PASSES):
            nc.vector.tensor_copy(
                out=x_plane[:, :, g, :].rearrange("p e (q b) -> p b q e", b=BATCH),
                in_=x_plane_in[:, g, :].rearrange("p (b q e) -> p b q e", b=BATCH, e=PARITY),
            )
            for b in range(BATCH):
                nc.vector.tensor_copy(
                    out=x_codes[:, :, g, :].rearrange("p e (q b y) -> p b q e y", b=BATCH, y=2)[:, b],
                    in_=x_codes_in[:, g, 2 * P * b : 2 * P * (b + 1)].rearrange(
                        "p (q e y) -> p q e y", e=PARITY, y=2
                    ),
                )

        for c in (2, 3):
            nc.vector.memset(w_plane[c][:].bitcast(I32), 0)
        load_chunk(2)

        nc.scalar.activation(out=warm[:], in_=zero[:], func=ACT.Sin)
        ratio = 10000.0 ** (-1.0 / PAIRS)
        width = 1
        while width < PAIRS:
            nc.scalar.activation(
                out=angle[:, :, width : 2 * width], in_=angle[:, :, 0:width], func=ACT.Copy,
                scale=ratio ** width,
            )
            width *= 2
        nc.scalar.activation(
            out=fold[:, 0], in_=angle[:], func=ACT.Abs, bias=1.5 * math.pi - 32.0 * math.pi, scale=1.0
        )
        nc.scalar.activation(out=fold[:, 1], in_=angle[:], func=ACT.Abs, bias=-32.0 * math.pi, scale=1.0)
        for half_range in (16.0, 8.0, 4.0, 2.0, 1.0):
            nc.scalar.activation(
                out=fold[:], in_=fold[:], func=ACT.Abs, bias=-half_range * math.pi, scale=1.0
            )
        nc.scalar.activation(
            out=cos_tab[:], in_=fold[:, 1].unsqueeze(3).to_broadcast([P, PARITY, PAIRS, 2]),
            func=ACT.Sin, bias=-0.5 * math.pi, scale=1.0,
        )
        nc.scalar.activation(out=sin_tab[:, 0], in_=fold[:, 0], func=ACT.Sin, bias=0.5 * math.pi, scale=-1.0)
        nc.scalar.activation(out=sin_tab[:, 1], in_=fold[:, 0], func=ACT.Sin, bias=-0.5 * math.pi, scale=1.0)

        chunk_of = {}
        for c, (first, n) in enumerate(CHUNKS):
            for k in range(n):
                chunk_of[first + k] = (c, k)

        def store(dest, shard, res, b):
            nc.sync.dma_start(
                out=dest[b, HEADS * shard : HEADS * (shard + 1), :, :].rearrange(
                    "h (q e) c -> q h (e c)", e=PARITY
                ),
                in_=res[b:P:BATCH].rearrange("p h e c -> p h (e c)"),
            )

        held = []
        for j in BLOCK_ORDER:
            c, k = chunk_of[j]
            shard, kind = divmod(j, 3)
            dest = (out_q, out_v, out_k)[kind]
            res = outs.tile([P, HEADS, PARITY, HEAD_DIM], F32, name="res", align_bytes=4096)
            for e in range(PARITY):
                acc = psum.tile([P, BLOCK], F32, name="acc")
                for g in range(PASSES):
                    nc.tensor.matmul_mx(
                        out=acc[:],
                        lhsT=x_codes[:, e, g, :].bitcast(FP4X4),
                        lhsT_scale=x_plane[:, e, g, :],
                        rhs=w_codes[c][:, g, 2 * BLOCK * k : 2 * BLOCK * (k + 1)].bitcast(FP4X4),
                        rhs_scale=w_plane[c][:, g, BLOCK * k : BLOCK * (k + 1)],
                        start=(g == 0),
                        stop=(g == PASSES - 1),
                    )
                x = acc[:].rearrange("p (h c) -> p h c", h=HEADS)
                if kind == 1:
                    if j == BLOCK_ORDER[-1] and e == 1:
                        nc.vector.tensor_copy(out=res[:, :, e, :], in_=x)
                    else:
                        nc.scalar.copy(out=res[:, :, e, :], in_=x)
                else:
                    cos_b = (
                        cos_tab[:, e].rearrange("p i x -> p (i x)").unsqueeze(1).to_broadcast([P, HEADS, ROT])
                    )
                    nsin_b = sin_tab[:, 0, e, :].unsqueeze(1).to_broadcast([P, HEADS, PAIRS])
                    psin_b = sin_tab[:, 1, e, :].unsqueeze(1).to_broadcast([P, HEADS, PAIRS])
                    cross = work.tile([P, HEADS, 2, PAIRS], F32, name="cross")
                    nc.scalar.copy(out=res[:, :, e, ROT:HEAD_DIM], in_=x[:, :, ROT:HEAD_DIM])
                    nc.vector.tensor_tensor(out=res[:, :, e, 0:ROT], in0=x[:, :, 0:ROT], in1=cos_b, op=ALU.mult)
                    nc.vector.tensor_tensor(out=cross[:, :, 0, :], in0=x[:, :, 1:ROT:2], in1=nsin_b, op=ALU.mult)
                    nc.vector.tensor_tensor(out=cross[:, :, 1, :], in0=x[:, :, 0:ROT:2], in1=psin_b, op=ALU.mult)
                    rot = res[:, :, e, 0:ROT].rearrange("p h (i x) -> p h i x", x=2)
                    nc.gpsimd.tensor_tensor(
                        out=rot, in0=rot, in1=cross[:].rearrange("p h x i -> p h i x"), op=ALU.add
                    )
            if j in BLOCK_ORDER[0:2]:
                held.append((dest, shard, res))
                if len(held) == 2:
                    for g in range(PASSES):
                        load_quarter(3, g)
                        held_dest, held_shard, held_res = held[g // BATCH]
                        store(held_dest, held_shard, held_res, g % BATCH)
            else:
                for b in range(BATCH):
                    store(dest, shard, res, b)
